import numpy as np
import ml_dtypes


def mxq(x, axis, fmt="e4m3"):
    dtype, down = {"e4m3": (ml_dtypes.float8_e4m3fn, 7), "e5m2": (ml_dtypes.float8_e5m2, 14)}[fmt]
    v = np.moveaxis(np.asarray(x, np.float32).astype(ml_dtypes.bfloat16).astype(np.float64), axis, -1)
    blocks = v.reshape(v.shape[:-1] + (-1, 32))
    amax = np.abs(blocks).max(-1, keepdims=True)
    byte = np.maximum(np.where(amax > 0, np.frexp(amax)[1] - 1 + 127, 0) - down, 1)
    scale = np.exp2(byte - 127.0)
    codes = (blocks / scale).astype(np.float32).astype(dtype).astype(np.float64)
    return np.moveaxis((codes * scale).reshape(v.shape), -1, axis)


WIDE = False


def mx_kscale(k):
    if not WIDE:
        return np.ones(k)
    levels = np.array([10, -10, 5, -5, 0])
    a = np.random.permutation(np.resize(levels, k // 512 * 4)).reshape(k // 512, 4)
    idx = np.arange(k)
    return np.exp2(a[idx // 512, idx % 128 // 32])


BF16 = ml_dtypes.bfloat16


def bf(x):
    return np.asarray(x, np.float32).astype(BF16)


def f64(x):
    return np.asarray(x).astype(np.float64)


B, S, M, H, KV, HD = 2, 2048, 1024, 4, 4, 128
E = H * HD


def sigmoid(v):
    return 1.0 / (1.0 + np.exp(-v))


def setup_inputs():
    s, t = mx_kscale(M), mx_kscale(E)
    return {"hidden_states": bf(np.random.standard_normal((B, S, M)) * s),
            "Wq_gate": bf(np.random.standard_normal((M, H, HD)) / np.sqrt(M) / s[:, None, None]),
            "attn": bf(np.random.standard_normal((B, S, H, HD)) * 0.5 * t.reshape(H, HD)),
            "Wo": bf(np.random.standard_normal((H, HD, M)) * 2.0 / np.sqrt(E) / t.reshape(H, HD, 1))}


def reference(hidden_states, Wq_gate, attn, Wo):
    gate = mxq(f64(hidden_states).reshape(B * S, M), 1, "e4m3") @ mxq(f64(Wq_gate).reshape(M, E), 0, "e4m3")
    g = f64(attn).reshape(B * S, E) * sigmoid(gate)
    return (mxq(g, 1, "e4m3") @ mxq(f64(Wo).reshape(E, M), 0, "e4m3")).reshape(B, S, M)

@@ -1,0 +1,300 @@
+from contextlib import ExitStack
+
+import concourse.mybir as mybir
+from concourse.masks import make_identity
+
+FLOPS = 2 * 4096 * 1024 * 512 * 2
+
+BF16 = mybir.dt.bfloat16
+F32 = mybir.dt.float32
+U32 = mybir.dt.uint32
+U8 = mybir.dt.uint8
+FP8X4 = mybir.dt.float8_e4m3fn_x4
+SIGMOID = mybir.ActivationFunctionType.Sigmoid
+MULT = mybir.AluOpType.mult
+
+P = 128
+TILES = 32
+UNITS = 16
+CHUNKS = (1, 1, 1, 1, 2, 2, 4, 4)
+
+
+def tile_qwen3_5attention_pb_t_kernel(tc, hidden_states, Wq_gate, attn, Wo, out):
+    nc = tc.nc
+    x_v = hidden_states.flatten_outer_dims().rearrange("(p j) m -> p j m", j=TILES)
+    a_v = attn.rearrange("b s u h -> (b s) (u h)").rearrange("(p j) e -> p j e", j=TILES)
+    o_v = out.flatten_outer_dims().rearrange("(p j) m -> p j m", j=TILES)
+    wq_v = Wq_gate.rearrange("(a q e) u h -> q a (e u h)", a=4, q=P, e=2)
+    wo_v = Wo.rearrange("u h m -> (u h) m").rearrange("(c q e) m -> q c (e m)", c=2, q=P, e=2)
+
+    with ExitStack() as ctx:
+        const = ctx.enter_context(tc.tile_pool(name="const", bufs=1))
+        resident = ctx.enter_context(tc.tile_pool(name="resident", bufs=1))
+        big = ctx.enter_context(tc.tile_pool(name="big", bufs=8))
+        work = ctx.enter_context(tc.tile_pool(name="work", bufs=2))
+        xt_pool = ctx.enter_context(tc.psum_pool(name="xt", bufs=2))
+        at_pool = ctx.enter_context(tc.psum_pool(name="at", bufs=1))
+        gate_pool = ctx.enter_context(tc.psum_pool(name="gate", bufs=2))
+        ob_pool = ctx.enter_context(tc.psum_pool(name="ob", bufs=3))
+        ctx.enter_context(tc.manual_schedule())
+
+        warm = const.tile([P, 1], F32, name="warm")
+        warm_out = const.tile([P, 1], F32, name="warm_out")
+        nc.vector.memset(warm[:], 0.0)
+        nc.scalar.activation(out=warm_out[:], in_=warm[:], func=SIGMOID)
+        ident = const.tile([P, P], F32, name="ident")
+        make_identity(nc, ident[:])
+
+        wqc = const.tile([P, 1024], U32, name="wqc", align_bytes=64)
+        wqs = const.tile([P, 1024], U8, name="wqs", align_bytes=64)
+        woc = const.tile([P, 1024], U32, name="woc", align_bytes=64)
+        wos = const.tile([P, 1024], U8, name="wos", align_bytes=64)
+
+        wq_raw = big.tile([P, 4096], BF16, name="wq_raw", tag="big", align_bytes=64)
+        wo_raw = big.tile([P, 4096], BF16, name="wo_raw", tag="big", align_bytes=64)
+        x_words = {}
+        a_words = {}
+        chunk_tiles = []
+        first = 0
+        for ci, units in enumerate(CHUNKS):
+            x_sb = resident.tile([P, units * 2048], BF16, name="x%d" % ci)
+            a_sb = resident.tile([P, units * 1024], BF16, name="a%d" % ci)
+            chunk_tiles.append((x_sb, a_sb, first, units))
+            for k in range(units):
+                x_words[first + k] = (x_sb, k * 1024)
+                a_words[first + k] = (a_sb, k * 512)
+            first += units
+
+        def load_x(ci):
+            x_sb, a_sb, u0, units = chunk_tiles[ci]
+            nc.sync.dma_start(
+                out=x_sb[:].rearrange("p (j m) -> p j m", j=2 * units),
+                in_=x_v[:, 2 * u0 : 2 * (u0 + units), :],
+            )
+
+        def load_a(ci):
+            x_sb, a_sb, u0, units = chunk_tiles[ci]
+            nc.sync.dma_start(
+                out=a_sb[:].rearrange("p (j e) -> p j e", j=2 * units),
+                in_=a_v[:, 2 * u0 : 2 * (u0 + units), :],
+            )
+
+        for g in range(2):
+            nc.sync.dma_start(
+                out=wq_raw[:, g * 2048 : (g + 1) * 2048].rearrange("p (a n) -> p a n", a=2),
+                in_=wq_v[:, 2 * g : 2 * g + 2, :],
+            )
+        load_x(0)
+        load_x(1)
+        nc.sync.dma_start(out=wo_raw[:].rearrange("p (c n) -> p c n", c=2), in_=wo_v)
+        load_a(0)
+        load_x(2)
+        load_a(1)
+        load_x(3)
+        load_a(2)
+        load_a(3)
+        for ci in range(4, len(CHUNKS)):
+            load_x(ci)
+            load_a(ci)
+
+        st = {}
+
+        def transpose_x(n):
+            x_sb, base = x_words[n]
+            xw = x_sb[:].bitcast(F32)
+            for g in range(2):
+                xt = xt_pool.tile([P, 512], F32, name="xt")
+                for u in range(2):
+                    for tt in range(2):
+                        col = base + tt * 512 + (2 * g + u) * P
+                        dst = u * 256 + tt * P
+                        nc.tensor.transpose(xt[:, dst : dst + P], xw[:, col : col + P], ident[:])
+                st["xt", n, g] = xt
+
+        def transpose_a(n):
+            a_sb, base = a_words[n]
+            aw = a_sb[:].bitcast(F32)
+            if n == UNITS - 1:
+                at = xt_pool.tile([P, 512], F32, name="xt")
+            else:
+                at = at_pool.tile([P, 512], F32, name="at")
+            for c in range(2):
+                for tt in range(2):
+                    col = base + tt * 256 + c * P
+                    dst = c * 256 + tt * P
+                    nc.tensor.transpose(at[:, dst : dst + P], aw[:, col : col + P], ident[:])
+            st["at", n] = at
+
+        def copy_xt(n, g, on_scalar):
+            if g == 0:
+                xg_new = work.tile([P, 2048], BF16, name="xg", align_bytes=64)
+                st["xg", n] = xg_new
+            xg = st["xg", n]
+            src = st["xt", n, g][:].rearrange("p (u t) -> p t u", u=2)
+            dst = xg[:].bitcast(F32)[:, g * 512 : (g + 1) * 512].rearrange("p (t u) -> p t u", u=2)
+            if on_scalar:
+                nc.scalar.copy(out=dst, in_=src)
+            else:
+                nc.vector.tensor_copy(out=dst, in_=src)
+
+        def quant_x(n):
+            xc = work.tile([P, 512], U32, name="xc", align_bytes=64)
+            xs = work.tile([P, 512], U8, name="xs", align_bytes=64)
+            nc.vector.quantize_mx(out=xc[:].bitcast(FP8X4), scales=xs[:], in_=st["xg", n][:])
+            st["xc", n] = (xc, xs)
+
+        def gate_mm(n, c):
+            xc, xs = st["xc", n]
+            gt = gate_pool.tile([P, 512], F32, name="gt")
+            for e in range(2):
+                for g in range(2):
+                    w0 = g * 512 + (e * 2 + c) * P
+                    nc.tensor.matmul_mx(
+                        out=gt[:, e * 256 : (e + 1) * 256],
+                        lhsT=wqc[:, w0 : w0 + P].bitcast(FP8X4),
+                        lhsT_scale=wqs[:, w0 : w0 + P],
+                        rhs=xc[:, g * 256 : (g + 1) * 256].bitcast(FP8X4),
+                        rhs_scale=xs[:, g * 256 : (g + 1) * 256],
+                        start=(g == 0),
+                        stop=(g == 1),
+                    )
+            st["gt", n, c] = gt
+
+        def sigmoid(n, c):
+            if c == 0:
+                sig_new = work.tile([P, 1024], F32, name="sig")
+                st["sig", n] = sig_new
+            sig = st["sig", n]
+            nc.scalar.activation(
+                out=sig[:, c * 512 : (c + 1) * 512].rearrange("p (t e) -> p t e", e=2),
+                in_=st["gt", n, c][:].rearrange("p (e t) -> p t e", e=2),
+                func=SIGMOID,
+            )
+
+        def multiply(n):
+            gg = work.tile([P, 1024], BF16, name="gg", align_bytes=64)
+            nc.vector.tensor_tensor(
+                out=gg[:].rearrange("p (t c e) -> p t c e", c=2, e=2),
+                in0=st["sig", n][:].rearrange("p (c t e) -> p t c e", c=2, e=2),
+                in1=st["at", n][:].bitcast(BF16).rearrange("p (c t e) -> p t c e", c=2, e=2),
+                op=MULT,
+            )
+            st["gg", n] = gg
+
+        def quant_g(n):
+            gc = work.tile([P, 256], U32, name="gc", align_bytes=64)
+            gs = work.tile([P, 256], U8, name="gs", align_bytes=64)
+            nc.vector.quantize_mx(out=gc[:].bitcast(FP8X4), scales=gs[:], in_=st["gg", n][:])
+            st["gc", n] = (gc, gs)
+
+        def out_mm(n, k):
+            gc, gs = st["gc", n]
+            tt, mh = divmod(k, 2)
+            ob = ob_pool.tile([P, 512], F32, name="ob")
+            nc.tensor.matmul_mx(
+                out=ob[:],
+                lhsT=gc[:, tt * P : (tt + 1) * P].bitcast(FP8X4),
+                lhsT_scale=gs[:, tt * P : (tt + 1) * P],
+                rhs=woc[:, mh * 512 : (mh + 1) * 512].bitcast(FP8X4),
+                rhs_scale=wos[:, mh * 512 : (mh + 1) * 512],
+                start=True,
+                stop=True,
+            )
+            st["ob", n, k] = ob
+
+        def copy_out(n, k, on_scalar):
+            if k == 0:
+                o_new = big.tile([P, 2048], F32, name="o", tag="big", align_bytes=64)
+                st["o", n] = o_new
+            dst = st["o", n][:, k * 512 : (k + 1) * 512]
+            if on_scalar:
+                nc.scalar.copy(out=dst, in_=st["ob", n, k][:])
+            else:
+                nc.vector.tensor_copy(out=dst, in_=st["ob", n, k][:])
+
+        def store(n):
+            nc.sync.dma_start(
+                out=o_v[:, 2 * n : 2 * n + 2, :],
+                in_=st["o", n][:].rearrange("p (j m) -> p j m", j=2),
+            )
+
+        def store_half(n, tt):
+            nc.sync.dma_start(
+                out=o_v[:, 2 * n + tt, :],
+                in_=st["o", n][:, tt * 1024 : (tt + 1) * 1024],
+            )
+
+        wq_grp = big.tile([P, 4096], BF16, name="wq_grp", tag="big", align_bytes=64)
+        wo_grp = big.tile([P, 4096], BF16, name="wo_grp", tag="big", align_bytes=64)
+        for g in range(2):
+            nc.vector.tensor_copy(
+                out=wq_grp[:, g * 2048 : (g + 1) * 2048].rearrange("p (e n j) -> p e n j", e=2, j=4),
+                in_=wq_raw[:, g * 2048 : (g + 1) * 2048].rearrange("p (j n e) -> p e n j", j=4, e=2),
+            )
+        nc.vector.quantize_mx(out=wqc[:].bitcast(FP8X4), scales=wqs[:], in_=wq_grp[:])
+        transpose_x(0)
+        copy_xt(0, 0, True)
+        copy_xt(0, 1, True)
+        quant_x(0)
+
+        transpose_x(1)
+        copy_xt(1, 0, True)
+        copy_xt(1, 1, True)
+        quant_x(1)
+
+        def regroup_wo(mh, on_scalar):
+            rows = wo_raw[:].rearrange("p (j m) -> p j m", j=4)[:, :, mh * 512 : (mh + 1) * 512]
+            src = rows.rearrange("p j (c i) -> p c j i", i=4)
+            dst = wo_grp[:, mh * 2048 : (mh + 1) * 2048].rearrange("p (c i j) -> p c j i", i=4, j=4)
+            if on_scalar:
+                nc.scalar.copy(out=dst, in_=src)
+            else:
+                nc.vector.tensor_copy(out=dst, in_=src)
+
+        def quant_wo(mh):
+            nc.vector.quantize_mx(
+                out=woc[:, mh * 512 : (mh + 1) * 512].bitcast(FP8X4),
+                scales=wos[:, mh * 512 : (mh + 1) * 512],
+                in_=wo_grp[:, mh * 2048 : (mh + 1) * 2048],
+            )
+
+        regroup_wo(0, False)
+        quant_wo(0)
+
+        for n in range(UNITS + 1):
+            if n >= 2:
+                out_mm(n - 2, 3)
+                copy_out(n - 2, 3, True)
+                store(n - 2)
+            if n < UNITS:
+                gate_mm(n, 0)
+                sigmoid(n, 0)
+                gate_mm(n, 1)
+                sigmoid(n, 1)
+            if n == 0:
+                regroup_wo(1, True)
+            if 1 <= n < UNITS:
+                for k in range(3):
+                    out_mm(n - 1, k)
+                    copy_out(n - 1, k, n < UNITS - 2 or k != 1)
+            if n == UNITS:
+                for k in range(4):
+                    out_mm(n - 1, k)
+                    copy_out(n - 1, k, k % 2 == 0)
+                    if k % 2 == 1:
+                        store_half(n - 1, k // 2)
+            if n < UNITS - 1:
+                transpose_a(n)
+            if n == UNITS - 2:
+                transpose_a(n + 1)
+            if n + 2 < UNITS:
+                transpose_x(n + 2)
+            if n < UNITS:
+                multiply(n)
+                quant_g(n)
+            if n == 0:
+                quant_wo(1)
+            if n + 2 < UNITS:
+                copy_xt(n + 2, 0, False)
+                copy_xt(n + 2, 1, False)
+                quant_x(n + 2)

@@ -32,6 +32,7 @@ def tile_qwen3_5attention_pb_t_kernel(tc, hidden_states, Wq_gate, attn, Wo, out)
         resident = ctx.enter_context(tc.tile_pool(name="resident", bufs=1))
         big = ctx.enter_context(tc.tile_pool(name="big", bufs=8))
         work = ctx.enter_context(tc.tile_pool(name="work", bufs=2))
+        work3 = ctx.enter_context(tc.tile_pool(name="work3", bufs=3))
         xt_pool = ctx.enter_context(tc.psum_pool(name="xt", bufs=2))
         at_pool = ctx.enter_context(tc.psum_pool(name="at", bufs=1))
         gate_pool = ctx.enter_context(tc.psum_pool(name="gate", bufs=2))
@@ -86,9 +87,9 @@ def tile_qwen3_5attention_pb_t_kernel(tc, hidden_states, Wq_gate, attn, Wo, out)
             )
         load_x(0)
         load_x(1)
-        nc.sync.dma_start(out=wo_raw[:].rearrange("p (c n) -> p c n", c=2), in_=wo_v)
-        load_a(0)
         load_x(2)
+        load_a(0)
+        nc.sync.dma_start(out=wo_raw[:].rearrange("p (c n) -> p c n", c=2), in_=wo_v)
         load_a(1)
         load_x(3)
         load_a(2)
@@ -182,8 +183,8 @@ def tile_qwen3_5attention_pb_t_kernel(tc, hidden_states, Wq_gate, attn, Wo, out)
             st["gg", n] = gg
 
         def quant_g(n):
-            gc = work.tile([P, 256], U32, name="gc", align_bytes=64)
-            gs = work.tile([P, 256], U8, name="gs", align_bytes=64)
+            gc = work3.tile([P, 256], U32, name="gc", align_bytes=64)
+            gs = work3.tile([P, 256], U8, name="gs", align_bytes=64)
             nc.vector.quantize_mx(out=gc[:].bitcast(FP8X4), scales=gs[:], in_=st["gg", n][:])
             st["gc", n] = (gc, gs)
 
@@ -232,16 +233,6 @@ def tile_qwen3_5attention_pb_t_kernel(tc, hidden_states, Wq_gate, attn, Wo, out)
                 in_=wq_raw[:, g * 2048 : (g + 1) * 2048].rearrange("p (j n e) -> p e n j", j=4, e=2),
             )
         nc.vector.quantize_mx(out=wqc[:].bitcast(FP8X4), scales=wqs[:], in_=wq_grp[:])
-        transpose_x(0)
-        copy_xt(0, 0, True)
-        copy_xt(0, 1, True)
-        quant_x(0)
-
-        transpose_x(1)
-        copy_xt(1, 0, True)
-        copy_xt(1, 1, True)
-        quant_x(1)
-
         def regroup_wo(mh, on_scalar):
             rows = wo_raw[:].rearrange("p (j m) -> p j m", j=4)[:, :, mh * 512 : (mh + 1) * 512]
             src = rows.rearrange("p j (c i) -> p c j i", i=4)
@@ -258,43 +249,52 @@ def tile_qwen3_5attention_pb_t_kernel(tc, hidden_states, Wq_gate, attn, Wo, out)
                 in_=wo_grp[:, mh * 2048 : (mh + 1) * 2048],
             )
 
-        regroup_wo(0, False)
-        quant_wo(0)
-
-        for n in range(UNITS + 1):
-            if n >= 2:
-                out_mm(n - 2, 3)
-                copy_out(n - 2, 3, True)
-                store(n - 2)
-            if n < UNITS:
-                gate_mm(n, 0)
-                sigmoid(n, 0)
-                gate_mm(n, 1)
-                sigmoid(n, 1)
-            if n == 0:
+        for i in range(-2, UNITS + 3):
+            a = i - 3
+            b = i - 2
+            d = i + 2
+            gated = 0 <= i < UNITS
+            late = a >= UNITS - 3
+            if 0 <= a:
+                copy_out(a, 0, True)
+                copy_out(a, 1, not late)
+                if a == UNITS - 1:
+                    store_half(a, 0)
+                copy_out(a, 2, True)
+            if gated:
+                gate_mm(i, 0)
+                gate_mm(i, 1)
+                sigmoid(i, 0)
+                sigmoid(i, 1)
+            if 0 <= a:
+                out_mm(a, 3)
+                copy_out(a, 3, False)
+                if a == UNITS - 1:
+                    store_half(a, 1)
+                else:
+                    store(a)
+            if d < UNITS:
+                transpose_x(d)
+            if gated and i < UNITS - 1:
+                transpose_a(i)
+            if i == UNITS - 2:
+                transpose_a(i + 1)
+            if d < UNITS:
+                copy_xt(d, 0, True)
+                copy_xt(d, 1, False)
+            if i == 0:
                 regroup_wo(1, True)
-            if 1 <= n < UNITS:
+            if 0 <= b < UNITS:
                 for k in range(3):
-                    out_mm(n - 1, k)
-                    copy_out(n - 1, k, n < UNITS - 2 or k != 1)
-            if n == UNITS:
-                for k in range(4):
-                    out_mm(n - 1, k)
-                    copy_out(n - 1, k, k % 2 == 0)
-                    if k % 2 == 1:
-                        store_half(n - 1, k // 2)
-            if n < UNITS - 1:
-                transpose_a(n)
-            if n == UNITS - 2:
-                transpose_a(n + 1)
-            if n + 2 < UNITS:
-                transpose_x(n + 2)
-            if n < UNITS:
-                multiply(n)
-                quant_g(n)
-            if n == 0:
+                    out_mm(b, k)
+            if gated:
+                multiply(i)
+            if d < UNITS:
+                quant_x(d)
+            if gated:
+                quant_g(i)
+            if i == 0:
+                regroup_wo(0, False)
+            if i == 1:
+                quant_wo(0)
                 quant_wo(1)
-            if n + 2 < UNITS:
-                copy_xt(n + 2, 0, False)
-                copy_xt(n + 2, 1, False)
-                quant_x(n + 2)

@@ -260,7 +260,7 @@ def tile_qwen3_5attention_pb_t_kernel(tc, hidden_states, Wq_gate, attn, Wo, out)
                 copy_out(a, 1, not late)
                 if a == UNITS - 1:
                     store_half(a, 0)
-                copy_out(a, 2, True)
+                copy_out(a, 2, a % 2 == 0)
             if gated:
                 gate_mm(i, 0)
                 gate_mm(i, 1)
@@ -281,7 +281,7 @@ def tile_qwen3_5attention_pb_t_kernel(tc, hidden_states, Wq_gate, attn, Wo, out)
                 transpose_a(i + 1)
             if d < UNITS:
                 copy_xt(d, 0, True)
-                copy_xt(d, 1, False)
+                copy_xt(d, 1, d < 2)
             if i == 0:
                 regroup_wo(1, True)
             if 0 <= b < UNITS:

@@ -32,7 +32,6 @@ def tile_qwen3_5attention_pb_t_kernel(tc, hidden_states, Wq_gate, attn, Wo, out)
         resident = ctx.enter_context(tc.tile_pool(name="resident", bufs=1))
         big = ctx.enter_context(tc.tile_pool(name="big", bufs=8))
         work = ctx.enter_context(tc.tile_pool(name="work", bufs=2))
-        work3 = ctx.enter_context(tc.tile_pool(name="work3", bufs=3))
         xt_pool = ctx.enter_context(tc.psum_pool(name="xt", bufs=2))
         at_pool = ctx.enter_context(tc.psum_pool(name="at", bufs=1))
         gate_pool = ctx.enter_context(tc.psum_pool(name="gate", bufs=2))
@@ -87,9 +86,9 @@ def tile_qwen3_5attention_pb_t_kernel(tc, hidden_states, Wq_gate, attn, Wo, out)
             )
         load_x(0)
         load_x(1)
+        nc.sync.dma_start(out=wo_raw[:].rearrange("p (c n) -> p c n", c=2), in_=wo_v)
         load_x(2)
         load_a(0)
-        nc.sync.dma_start(out=wo_raw[:].rearrange("p (c n) -> p c n", c=2), in_=wo_v)
         load_a(1)
         load_x(3)
         load_a(2)
@@ -183,15 +182,18 @@ def tile_qwen3_5attention_pb_t_kernel(tc, hidden_states, Wq_gate, attn, Wo, out)
             st["gg", n] = gg
 
         def quant_g(n):
-            gc = work3.tile([P, 256], U32, name="gc", align_bytes=64)
-            gs = work3.tile([P, 256], U8, name="gs", align_bytes=64)
+            gc = work.tile([P, 256], U32, name="gc", align_bytes=64)
+            gs = work.tile([P, 256], U8, name="gs", align_bytes=64)
             nc.vector.quantize_mx(out=gc[:].bitcast(FP8X4), scales=gs[:], in_=st["gg", n][:])
             st["gc", n] = (gc, gs)
 
-        def out_mm(n, k):
+        def out_mm(n, k, in_gate_bank=False):
             gc, gs = st["gc", n]
             tt, mh = divmod(k, 2)
-            ob = ob_pool.tile([P, 512], F32, name="ob")
+            if in_gate_bank:
+                ob = gate_pool.tile([P, 512], F32, name="gt")
+            else:
+                ob = ob_pool.tile([P, 512], F32, name="ob")
             nc.tensor.matmul_mx(
                 out=ob[:],
                 lhsT=gc[:, tt * P : (tt + 1) * P].bitcast(FP8X4),
@@ -249,52 +251,91 @@ def tile_qwen3_5attention_pb_t_kernel(tc, hidden_states, Wq_gate, attn, Wo, out)
                 in_=wo_grp[:, mh * 2048 : (mh + 1) * 2048],
             )
 
-        for i in range(-2, UNITS + 3):
-            a = i - 3
-            b = i - 2
+        for i in range(-2, UNITS - 2):
+            a = i - 2
+            b = i - 1
             d = i + 2
-            gated = 0 <= i < UNITS
-            late = a >= UNITS - 3
-            if 0 <= a:
+            if a >= 0:
                 copy_out(a, 0, True)
-                copy_out(a, 1, not late)
-                if a == UNITS - 1:
-                    store_half(a, 0)
-                copy_out(a, 2, a % 2 == 0)
-            if gated:
+                copy_out(a, 1, True)
+                copy_out(a, 2, True)
+            if i >= 0:
                 gate_mm(i, 0)
                 gate_mm(i, 1)
                 sigmoid(i, 0)
                 sigmoid(i, 1)
-            if 0 <= a:
+            if a >= 0:
                 out_mm(a, 3)
                 copy_out(a, 3, False)
-                if a == UNITS - 1:
-                    store_half(a, 1)
-                else:
-                    store(a)
-            if d < UNITS:
-                transpose_x(d)
-            if gated and i < UNITS - 1:
+                store(a)
+            transpose_x(d)
+            if i >= 0:
                 transpose_a(i)
-            if i == UNITS - 2:
-                transpose_a(i + 1)
-            if d < UNITS:
-                copy_xt(d, 0, True)
-                copy_xt(d, 1, d < 2)
+            copy_xt(d, 0, True)
+            copy_xt(d, 1, d < 2)
             if i == 0:
                 regroup_wo(1, True)
-            if 0 <= b < UNITS:
+            if b >= 0:
                 for k in range(3):
                     out_mm(b, k)
-            if gated:
+            if i >= 0:
                 multiply(i)
-            if d < UNITS:
-                quant_x(d)
-            if gated:
+            quant_x(d)
+            if i >= 0:
                 quant_g(i)
-            if i == 0:
+            if i == -1:
                 regroup_wo(0, False)
-            if i == 1:
                 quant_wo(0)
+            if i == 0:
                 quant_wo(1)
+
+        u = UNITS - 4
+        copy_out(u, 0, True)
+        copy_out(u, 1, True)
+        copy_out(u, 2, True)
+        gate_mm(u + 2, 0)
+        gate_mm(u + 2, 1)
+        sigmoid(u + 2, 0)
+        sigmoid(u + 2, 1)
+        out_mm(u, 3)
+        copy_out(u, 3, False)
+        store(u)
+        transpose_a(u + 2)
+        transpose_a(u + 3)
+        for k in range(3):
+            out_mm(u + 1, k)
+        multiply(u + 2)
+        quant_g(u + 2)
+
+        gate_mm(u + 3, 0)
+        gate_mm(u + 3, 1)
+        copy_out(u + 1, 0, True)
+        copy_out(u + 1, 1, True)
+        store_half(u + 1, 0)
+        copy_out(u + 1, 2, False)
+        sigmoid(u + 3, 0)
+        sigmoid(u + 3, 1)
+        out_mm(u + 1, 3)
+        copy_out(u + 1, 3, False)
+        store_half(u + 1, 1)
+        for k in range(3):
+            out_mm(u + 2, k)
+        multiply(u + 3)
+        quant_g(u + 3)
+
+        copy_out(u + 2, 0, True)
+        copy_out(u + 2, 1, True)
+        store_half(u + 2, 0)
+        out_mm(u + 2, 3, True)
+        copy_out(u + 2, 2, True)
+        copy_out(u + 2, 3, False)
+        store_half(u + 2, 1)
+        for k in range(3):
+            out_mm(u + 3, k)
+        out_mm(u + 3, 3, True)
+        copy_out(u + 3, 0, True)
+        copy_out(u + 3, 1, False)
+        store_half(u + 3, 0)
+        copy_out(u + 3, 2, True)
+        copy_out(u + 3, 3, False)
+        store_half(u + 3, 1)

@@ -16,6 +16,7 @@ MULT = mybir.AluOpType.mult
 P = 128
 TILES = 32
 UNITS = 16
+WARM = (4, 2, 2)
 CHUNKS = (1, 1, 1, 1, 2, 2, 4, 4)
 
 
@@ -251,6 +252,12 @@ def tile_qwen3_5attention_pb_t_kernel(tc, hidden_states, Wq_gate, attn, Wo, out)
                 in_=wo_grp[:, mh * 2048 : (mh + 1) * 2048],
             )
 
+        def warm_up(count):
+            for r in range(count):
+                dummy = ob_pool.tile([P, 512], F32, name="ob")
+                nc.tensor.matmul(out=dummy[:], lhsT=wq_raw[:, 0:P], rhs=wq_raw[:, 0:512], start=True, stop=True)
+
+        warm_up(WARM[0])
         for i in range(-2, UNITS - 2):
             a = i - 2
             b = i - 1
@@ -271,6 +278,8 @@ def tile_qwen3_5attention_pb_t_kernel(tc, hidden_states, Wq_gate, attn, Wo, out)
             transpose_x(d)
             if i >= 0:
                 transpose_a(i)
+            if i < 0:
+                warm_up(WARM[i + 3])
             copy_xt(d, 0, True)
             copy_xt(d, 1, d < 2)
             if i == 0:

@@ -17,7 +17,10 @@ P = 128
 TILES = 32
 UNITS = 16
 WARM = (4, 2, 2)
-CHUNKS = (1, 1, 1, 1, 2, 2, 4, 4)
+X_CHUNKS = (1, 1, 1, 1, 2, 4, 6)
+A_CHUNKS = (1, 1, 2, 2, 4, 6)
+FIRST = 4
+PAIRS = 10
 
 
 def tile_qwen3_5attention_pb_t_kernel(tc, hidden_states, Wq_gate, attn, Wo, out):
@@ -31,7 +34,8 @@ def tile_qwen3_5attention_pb_t_kernel(tc, hidden_states, Wq_gate, attn, Wo, out)
     with ExitStack() as ctx:
         const = ctx.enter_context(tc.tile_pool(name="const", bufs=1))
         resident = ctx.enter_context(tc.tile_pool(name="resident", bufs=1))
-        big = ctx.enter_context(tc.tile_pool(name="big", bufs=8))
+        first_pool = ctx.enter_context(tc.tile_pool(name="first", bufs=1))
+        pair_pool = ctx.enter_context(tc.tile_pool(name="pair", bufs=3))
         work = ctx.enter_context(tc.tile_pool(name="work", bufs=2))
         xt_pool = ctx.enter_context(tc.psum_pool(name="xt", bufs=2))
         at_pool = ctx.enter_context(tc.psum_pool(name="at", bufs=1))
@@ -51,30 +55,39 @@ def tile_qwen3_5attention_pb_t_kernel(tc, hidden_states, Wq_gate, attn, Wo, out)
         woc = const.tile([P, 1024], U32, name="woc", align_bytes=64)
         wos = const.tile([P, 1024], U8, name="wos", align_bytes=64)
 
-        wq_raw = big.tile([P, 4096], BF16, name="wq_raw", tag="big", align_bytes=64)
-        wo_raw = big.tile([P, 4096], BF16, name="wo_raw", tag="big", align_bytes=64)
+        staging = first_pool.tile([P, 16384], BF16, name="staging", tag="first", align_bytes=64)
+        wq_raw = staging[:, 0:4096]
+        wq_grp = staging[:, 4096:8192]
+        wo_raw = staging[:, 8192:12288]
+        wo_grp = staging[:, 12288:16384]
         x_words = {}
         a_words = {}
-        chunk_tiles = []
+        x_tiles = []
         first = 0
-        for ci, units in enumerate(CHUNKS):
+        for ci, units in enumerate(X_CHUNKS):
             x_sb = resident.tile([P, units * 2048], BF16, name="x%d" % ci)
-            a_sb = resident.tile([P, units * 1024], BF16, name="a%d" % ci)
-            chunk_tiles.append((x_sb, a_sb, first, units))
+            x_tiles.append((x_sb, first, units))
             for k in range(units):
                 x_words[first + k] = (x_sb, k * 1024)
+            first += units
+        a_tiles = []
+        first = 0
+        for ci, units in enumerate(A_CHUNKS):
+            a_sb = resident.tile([P, units * 1024], BF16, name="a%d" % ci)
+            a_tiles.append((a_sb, first, units))
+            for k in range(units):
                 a_words[first + k] = (a_sb, k * 512)
             first += units
 
         def load_x(ci):
-            x_sb, a_sb, u0, units = chunk_tiles[ci]
+            x_sb, u0, units = x_tiles[ci]
             nc.sync.dma_start(
                 out=x_sb[:].rearrange("p (j m) -> p j m", j=2 * units),
                 in_=x_v[:, 2 * u0 : 2 * (u0 + units), :],
             )
 
         def load_a(ci):
-            x_sb, a_sb, u0, units = chunk_tiles[ci]
+            a_sb, u0, units = a_tiles[ci]
             nc.sync.dma_start(
                 out=a_sb[:].rearrange("p (j e) -> p j e", j=2 * units),
                 in_=a_v[:, 2 * u0 : 2 * (u0 + units), :],
@@ -87,16 +100,15 @@ def tile_qwen3_5attention_pb_t_kernel(tc, hidden_states, Wq_gate, attn, Wo, out)
             )
         load_x(0)
         load_x(1)
-        nc.sync.dma_start(out=wo_raw[:].rearrange("p (c n) -> p c n", c=2), in_=wo_v)
+        nc.sync.dma_start(out=wo_raw.rearrange("p (c n) -> p c n", c=2), in_=wo_v)
         load_x(2)
         load_a(0)
         load_a(1)
         load_x(3)
         load_a(2)
-        load_a(3)
-        for ci in range(4, len(CHUNKS)):
+        for ci in range(4, len(X_CHUNKS)):
             load_x(ci)
-            load_a(ci)
+            load_a(ci - 1)
 
         st = {}
 
@@ -208,36 +220,43 @@ def tile_qwen3_5attention_pb_t_kernel(tc, hidden_states, Wq_gate, attn, Wo, out)
 
         def copy_out(n, k, on_scalar):
             if k == 0:
-                o_new = big.tile([P, 2048], F32, name="o", tag="big", align_bytes=64)
-                st["o", n] = o_new
-            dst = st["o", n][:, k * 512 : (k + 1) * 512]
+                if n == 0:
+                    o_first = first_pool.tile([P, FIRST * 2048], F32, name="o_first", tag="first", align_bytes=64)
+                    for r in range(FIRST):
+                        st["o", r] = (o_first, r * 2048)
+                elif n >= FIRST and n % 2 == 0:
+                    o_pair = pair_pool.tile([P, 4096], F32, name="o_pair", align_bytes=64)
+                    st["o", n] = (o_pair, 0)
+                    st["o", n + 1] = (o_pair, 2048)
+            o_sb, base = st["o", n]
+            dst = o_sb[:, base + k * 512 : base + (k + 1) * 512]
             if on_scalar:
                 nc.scalar.copy(out=dst, in_=st["ob", n, k][:])
             else:
                 nc.vector.tensor_copy(out=dst, in_=st["ob", n, k][:])
 
-        def store(n):
+        def store(n, units=1):
+            o_sb, base = st["o", n - units + 1]
             nc.sync.dma_start(
-                out=o_v[:, 2 * n : 2 * n + 2, :],
-                in_=st["o", n][:].rearrange("p (j m) -> p j m", j=2),
+                out=o_v[:, 2 * (n - units + 1) : 2 * n + 2, :],
+                in_=o_sb[:, base : base + units * 2048].rearrange("p (j m) -> p j m", j=2 * units),
             )
 
         def store_half(n, tt):
+            o_sb, base = st["o", n]
             nc.sync.dma_start(
                 out=o_v[:, 2 * n + tt, :],
-                in_=st["o", n][:, tt * 1024 : (tt + 1) * 1024],
+                in_=o_sb[:, base + tt * 1024 : base + (tt + 1) * 1024],
             )
 
-        wq_grp = big.tile([P, 4096], BF16, name="wq_grp", tag="big", align_bytes=64)
-        wo_grp = big.tile([P, 4096], BF16, name="wo_grp", tag="big", align_bytes=64)
         for g in range(2):
             nc.vector.tensor_copy(
                 out=wq_grp[:, g * 2048 : (g + 1) * 2048].rearrange("p (e n j) -> p e n j", e=2, j=4),
                 in_=wq_raw[:, g * 2048 : (g + 1) * 2048].rearrange("p (j n e) -> p e n j", j=4, e=2),
             )
-        nc.vector.quantize_mx(out=wqc[:].bitcast(FP8X4), scales=wqs[:], in_=wq_grp[:])
+        nc.vector.quantize_mx(out=wqc[:].bitcast(FP8X4), scales=wqs[:], in_=wq_grp)
         def regroup_wo(mh, on_scalar):
-            rows = wo_raw[:].rearrange("p (j m) -> p j m", j=4)[:, :, mh * 512 : (mh + 1) * 512]
+            rows = wo_raw.rearrange("p (j m) -> p j m", j=4)[:, :, mh * 512 : (mh + 1) * 512]
             src = rows.rearrange("p j (c i) -> p c j i", i=4)
             dst = wo_grp[:, mh * 2048 : (mh + 1) * 2048].rearrange("p (c i j) -> p c j i", i=4, j=4)
             if on_scalar:
@@ -274,7 +293,12 @@ def tile_qwen3_5attention_pb_t_kernel(tc, hidden_states, Wq_gate, attn, Wo, out)
             if a >= 0:
                 out_mm(a, 3)
                 copy_out(a, 3, False)
-                store(a)
+                if a == FIRST - 1:
+                    store(a, FIRST)
+                elif FIRST < a < PAIRS and a % 2 == 1:
+                    store(a, 2)
+                elif a >= PAIRS:
+                    store(a)
             transpose_x(d)
             if i >= 0:
                 transpose_a(i)

@@ -16,7 +16,6 @@ MULT = mybir.AluOpType.mult
 P = 128
 TILES = 32
 UNITS = 16
-WARM = (4, 2, 2)
 X_CHUNKS = (1, 1, 1, 1, 2, 4, 6)
 A_CHUNKS = (1, 1, 2, 2, 4, 6)
 FIRST = 4
@@ -93,18 +92,18 @@ def tile_qwen3_5attention_pb_t_kernel(tc, hidden_states, Wq_gate, attn, Wo, out)
                 in_=a_v[:, 2 * u0 : 2 * (u0 + units), :],
             )
 
+        load_x(0)
         for g in range(2):
             nc.sync.dma_start(
                 out=wq_raw[:, g * 2048 : (g + 1) * 2048].rearrange("p (a n) -> p a n", a=2),
                 in_=wq_v[:, 2 * g : 2 * g + 2, :],
             )
-        load_x(0)
         load_x(1)
         nc.sync.dma_start(out=wo_raw.rearrange("p (c n) -> p c n", c=2), in_=wo_v)
-        load_x(2)
         load_a(0)
-        load_a(1)
+        load_x(2)
         load_x(3)
+        load_a(1)
         load_a(2)
         for ci in range(4, len(X_CHUNKS)):
             load_x(ci)
@@ -200,10 +199,10 @@ def tile_qwen3_5attention_pb_t_kernel(tc, hidden_states, Wq_gate, attn, Wo, out)
             nc.vector.quantize_mx(out=gc[:].bitcast(FP8X4), scales=gs[:], in_=st["gg", n][:])
             st["gc", n] = (gc, gs)
 
-        def out_mm(n, k, in_gate_bank=False):
+        def out_mm(n, k, bank="ob"):
             gc, gs = st["gc", n]
             tt, mh = divmod(k, 2)
-            if in_gate_bank:
+            if bank == "gt":
                 ob = gate_pool.tile([P, 512], F32, name="gt")
             else:
                 ob = ob_pool.tile([P, 512], F32, name="ob")
@@ -249,12 +248,21 @@ def tile_qwen3_5attention_pb_t_kernel(tc, hidden_states, Wq_gate, attn, Wo, out)
                 in_=o_sb[:, base + tt * 1024 : base + (tt + 1) * 1024],
             )
 
-        for g in range(2):
-            nc.vector.tensor_copy(
-                out=wq_grp[:, g * 2048 : (g + 1) * 2048].rearrange("p (e n j) -> p e n j", e=2, j=4),
-                in_=wq_raw[:, g * 2048 : (g + 1) * 2048].rearrange("p (j n e) -> p e n j", j=4, e=2),
+        def regroup_wq(g, e, on_scalar):
+            src = wq_raw[:, g * 2048 : (g + 1) * 2048].rearrange("p (j n e) -> p e n j", j=4, e=2)[:, e, :, :]
+            dst = wq_grp[:, g * 2048 + e * 1024 : g * 2048 + (e + 1) * 1024].rearrange("p (n j) -> p n j", j=4)
+            if on_scalar:
+                nc.scalar.copy(out=dst, in_=src)
+            else:
+                nc.vector.tensor_copy(out=dst, in_=src)
+
+        def quant_wq(g):
+            nc.vector.quantize_mx(
+                out=wqc[:, g * 512 : (g + 1) * 512].bitcast(FP8X4),
+                scales=wqs[:, g * 512 : (g + 1) * 512],
+                in_=wq_grp[:, g * 2048 : (g + 1) * 2048],
             )
-        nc.vector.quantize_mx(out=wqc[:].bitcast(FP8X4), scales=wqs[:], in_=wq_grp)
+
         def regroup_wo(mh, on_scalar):
             rows = wo_raw.rearrange("p (j m) -> p j m", j=4)[:, :, mh * 512 : (mh + 1) * 512]
             src = rows.rearrange("p j (c i) -> p c j i", i=4)
@@ -271,60 +279,85 @@ def tile_qwen3_5attention_pb_t_kernel(tc, hidden_states, Wq_gate, attn, Wo, out)
                 in_=wo_grp[:, mh * 2048 : (mh + 1) * 2048],
             )
 
-        def warm_up(count):
-            for r in range(count):
-                dummy = ob_pool.tile([P, 512], F32, name="ob")
-                nc.tensor.matmul(out=dummy[:], lhsT=wq_raw[:, 0:P], rhs=wq_raw[:, 0:512], start=True, stop=True)
-
-        warm_up(WARM[0])
-        for i in range(-2, UNITS - 2):
+        transpose_x(0)
+        for r in range(4):
+            dummy = ob_pool.tile([P, 512], F32, name="ob")
+            nc.tensor.matmul(out=dummy[:], lhsT=wq_raw[:, 0:P], rhs=wq_raw[:, 0:512], start=True, stop=True)
+        copy_xt(0, 0, True)
+        copy_xt(0, 1, False)
+        regroup_wq(0, 0, False)
+        regroup_wq(0, 1, True)
+        quant_x(0)
+        regroup_wq(1, 0, False)
+        regroup_wq(1, 1, True)
+        quant_wq(0)
+        transpose_x(1)
+        copy_xt(1, 0, True)
+        copy_xt(1, 1, True)
+        quant_wq(1)
+        quant_x(1)
+        gate_mm(0, 0)
+        gate_mm(0, 1)
+        sigmoid(0, 0)
+        sigmoid(0, 1)
+        transpose_a(0)
+        regroup_wo(0, False)
+        regroup_wo(1, True)
+        gate_mm(1, 0)
+        gate_mm(1, 1)
+        multiply(0)
+        quant_wo(0)
+        quant_g(0)
+        transpose_x(2)
+        copy_xt(2, 0, True)
+        copy_xt(2, 1, False)
+        sigmoid(1, 0)
+        sigmoid(1, 1)
+        quant_wo(1)
+        quant_x(2)
+        out_mm(0, 0)
+        out_mm(0, 2)
+        transpose_x(3)
+        transpose_a(1)
+        copy_xt(3, 0, True)
+        copy_xt(3, 1, False)
+        out_mm(0, 1)
+        multiply(1)
+        quant_x(3)
+        quant_g(1)
+        for i in range(2, UNITS - 2):
             a = i - 2
             b = i - 1
             d = i + 2
-            if a >= 0:
-                copy_out(a, 0, True)
-                copy_out(a, 1, True)
-                copy_out(a, 2, True)
-            if i >= 0:
-                gate_mm(i, 0)
-                gate_mm(i, 1)
-                sigmoid(i, 0)
-                sigmoid(i, 1)
-            if a >= 0:
-                out_mm(a, 3)
-                copy_out(a, 3, False)
-                if a == FIRST - 1:
-                    store(a, FIRST)
-                elif FIRST < a < PAIRS and a % 2 == 1:
-                    store(a, 2)
-                elif a >= PAIRS:
-                    store(a)
+            copy_out(a, 0, True)
+            copy_out(a, 1, True)
+            copy_out(a, 2, True)
+            gate_mm(i, 0)
+            gate_mm(i, 1)
+            sigmoid(i, 0)
+            sigmoid(i, 1)
+            out_mm(a, 3)
+            copy_out(a, 3, False)
+            if a == FIRST - 1:
+                store(a, FIRST)
+            elif FIRST < a < PAIRS and a % 2 == 1:
+                store(a, 2)
+            elif a >= PAIRS:
+                store(a)
             transpose_x(d)
-            if i >= 0:
-                transpose_a(i)
-            if i < 0:
-                warm_up(WARM[i + 3])
+            transpose_a(i)
             copy_xt(d, 0, True)
-            copy_xt(d, 1, d < 2)
-            if i == 0:
-                regroup_wo(1, True)
-            if b >= 0:
-                for k in range(3):
-                    out_mm(b, k)
-            if i >= 0:
-                multiply(i)
+            copy_xt(d, 1, False)
+            for k in range(3):
+                out_mm(b, k)
+            multiply(i)
             quant_x(d)
-            if i >= 0:
-                quant_g(i)
-            if i == -1:
-                regroup_wo(0, False)
-                quant_wo(0)
-            if i == 0:
-                quant_wo(1)
+            quant_g(i)
 
         u = UNITS - 4
         copy_out(u, 0, True)
         copy_out(u, 1, True)
+        store_half(u, 0)
         copy_out(u, 2, True)
         gate_mm(u + 2, 0)
         gate_mm(u + 2, 1)
@@ -332,7 +365,7 @@ def tile_qwen3_5attention_pb_t_kernel(tc, hidden_states, Wq_gate, attn, Wo, out)
         sigmoid(u + 2, 1)
         out_mm(u, 3)
         copy_out(u, 3, False)
-        store(u)
+        store_half(u, 1)
         transpose_a(u + 2)
         transpose_a(u + 3)
         for k in range(3):
@@ -359,13 +392,13 @@ def tile_qwen3_5attention_pb_t_kernel(tc, hidden_states, Wq_gate, attn, Wo, out)
         copy_out(u + 2, 0, True)
         copy_out(u + 2, 1, True)
         store_half(u + 2, 0)
-        out_mm(u + 2, 3, True)
+        out_mm(u + 2, 3, "gt")
         copy_out(u + 2, 2, True)
         copy_out(u + 2, 3, False)
         store_half(u + 2, 1)
         for k in range(3):
             out_mm(u + 3, k)
-        out_mm(u + 3, 3, True)
+        out_mm(u + 3, 3, "gt")
         copy_out(u + 3, 0, True)
         copy_out(u + 3, 1, False)
         store_half(u + 3, 0)

@@ -17,9 +17,10 @@ P = 128
 TILES = 32
 UNITS = 16
 X_CHUNKS = (1, 1, 1, 1, 2, 4, 6)
-A_CHUNKS = (1, 1, 2, 2, 4, 6)
-FIRST = 4
-PAIRS = 10
+A_CHUNKS = (1, 3, 4, 8)
+FIRST = 5
+GROUP = 3
+STORES = {4: 5, 7: 3, 9: 2, 10: 1, 11: 1}
 
 
 def tile_qwen3_5attention_pb_t_kernel(tc, hidden_states, Wq_gate, attn, Wo, out):
@@ -34,7 +35,7 @@ def tile_qwen3_5attention_pb_t_kernel(tc, hidden_states, Wq_gate, attn, Wo, out)
         const = ctx.enter_context(tc.tile_pool(name="const", bufs=1))
         resident = ctx.enter_context(tc.tile_pool(name="resident", bufs=1))
         first_pool = ctx.enter_context(tc.tile_pool(name="first", bufs=1))
-        pair_pool = ctx.enter_context(tc.tile_pool(name="pair", bufs=3))
+        group_pool = ctx.enter_context(tc.tile_pool(name="group", bufs=2))
         work = ctx.enter_context(tc.tile_pool(name="work", bufs=2))
         xt_pool = ctx.enter_context(tc.psum_pool(name="xt", bufs=2))
         at_pool = ctx.enter_context(tc.psum_pool(name="at", bufs=1))
@@ -48,13 +49,15 @@ def tile_qwen3_5attention_pb_t_kernel(tc, hidden_states, Wq_gate, attn, Wo, out)
         nc.scalar.activation(out=warm_out[:], in_=warm[:], func=SIGMOID)
         ident = const.tile([P, P], F32, name="ident")
         make_identity(nc, ident[:])
+        zeros = const.tile([P, 512], BF16, name="zeros")
+        nc.vector.memset(zeros[:], 0.0)
 
         wqc = const.tile([P, 1024], U32, name="wqc", align_bytes=64)
         wqs = const.tile([P, 1024], U8, name="wqs", align_bytes=64)
         woc = const.tile([P, 1024], U32, name="woc", align_bytes=64)
         wos = const.tile([P, 1024], U8, name="wos", align_bytes=64)
 
-        staging = first_pool.tile([P, 16384], BF16, name="staging", tag="first", align_bytes=64)
+        staging = first_pool.tile([P, FIRST * 4096], BF16, name="staging", tag="first", align_bytes=64)
         wq_raw = staging[:, 0:4096]
         wq_grp = staging[:, 4096:8192]
         wo_raw = staging[:, 8192:12288]
@@ -104,10 +107,10 @@ def tile_qwen3_5attention_pb_t_kernel(tc, hidden_states, Wq_gate, attn, Wo, out)
         load_x(2)
         load_x(3)
         load_a(1)
-        load_a(2)
         for ci in range(4, len(X_CHUNKS)):
             load_x(ci)
-            load_a(ci - 1)
+            if ci < len(X_CHUNKS) - 1:
+                load_a(ci - 2)
 
         st = {}
 
@@ -172,6 +175,59 @@ def tile_qwen3_5attention_pb_t_kernel(tc, hidden_states, Wq_gate, attn, Wo, out)
                     )
             st["gt", n, c] = gt
 
+        def gate_mm_half(n, tt):
+            xc, xs = st["xc", n]
+            gt = gate_pool.tile([P, 512], F32, name="gt")
+            for c in range(2):
+                for e in range(2):
+                    for g in range(2):
+                        w0 = g * 512 + (e * 2 + c) * P
+                        t0 = g * 256 + tt * P
+                        nc.tensor.matmul_mx(
+                            out=gt[:, (2 * c + e) * P : (2 * c + e + 1) * P],
+                            lhsT=wqc[:, w0 : w0 + P].bitcast(FP8X4),
+                            lhsT_scale=wqs[:, w0 : w0 + P],
+                            rhs=xc[:, t0 : t0 + P].bitcast(FP8X4),
+                            rhs_scale=xs[:, t0 : t0 + P],
+                            start=(g == 0),
+                            stop=(g == 1),
+                        )
+            st["gt", n, tt] = gt
+
+        def sigmoid_half(n, tt):
+            if tt == 0:
+                sig_new = work.tile([P, 1024], F32, name="sig")
+                st["sig", n] = sig_new
+            nc.scalar.activation(
+                out=st["sig", n][:, tt * 512 : (tt + 1) * 512].rearrange("p (t c e) -> p t c e", c=2, e=2),
+                in_=st["gt", n, tt][:].rearrange("p (c e t) -> p t c e", c=2, e=2),
+                func=SIGMOID,
+            )
+
+        def multiply_half(n, tt):
+            if tt == 0:
+                gg_new = work.tile([P, 1024], BF16, name="gg", align_bytes=64)
+                st["gg", n] = gg_new
+            at = st["at", n][:].bitcast(BF16).rearrange("p (c t e) -> p t c e", c=2, e=2)
+            nc.vector.tensor_tensor(
+                out=st["gg", n][:, tt * 512 : (tt + 1) * 512].rearrange("p (t c e) -> p t c e", c=2, e=2),
+                in0=st["sig", n][:, tt * 512 : (tt + 1) * 512].rearrange("p (t c e) -> p t c e", c=2, e=2),
+                in1=at[:, tt * P : (tt + 1) * P, :, :],
+                op=MULT,
+            )
+
+        def quant_g_half(n, tt):
+            if tt == 0:
+                gc_new = work.tile([P, 256], U32, name="gc", align_bytes=64)
+                gs_new = work.tile([P, 256], U8, name="gs", align_bytes=64)
+                st["gc", n] = (gc_new, gs_new)
+            gc, gs = st["gc", n]
+            nc.vector.quantize_mx(
+                out=gc[:, tt * P : (tt + 1) * P].bitcast(FP8X4),
+                scales=gs[:, tt * P : (tt + 1) * P],
+                in_=st["gg", n][:, tt * 512 : (tt + 1) * 512],
+            )
+
         def sigmoid(n, c):
             if c == 0:
                 sig_new = work.tile([P, 1024], F32, name="sig")
@@ -204,6 +260,10 @@ def tile_qwen3_5attention_pb_t_kernel(tc, hidden_states, Wq_gate, attn, Wo, out)
             tt, mh = divmod(k, 2)
             if bank == "gt":
                 ob = gate_pool.tile([P, 512], F32, name="gt")
+            elif bank == "xt":
+                ob = xt_pool.tile([P, 512], F32, name="xt")
+            elif bank == "at":
+                ob = at_pool.tile([P, 512], F32, name="at")
             else:
                 ob = ob_pool.tile([P, 512], F32, name="ob")
             nc.tensor.matmul_mx(
@@ -223,10 +283,10 @@ def tile_qwen3_5attention_pb_t_kernel(tc, hidden_states, Wq_gate, attn, Wo, out)
                     o_first = first_pool.tile([P, FIRST * 2048], F32, name="o_first", tag="first", align_bytes=64)
                     for r in range(FIRST):
                         st["o", r] = (o_first, r * 2048)
-                elif n >= FIRST and n % 2 == 0:
-                    o_pair = pair_pool.tile([P, 4096], F32, name="o_pair", align_bytes=64)
-                    st["o", n] = (o_pair, 0)
-                    st["o", n + 1] = (o_pair, 2048)
+                elif n >= FIRST and (n - FIRST) % GROUP == 0:
+                    o_group = group_pool.tile([P, GROUP * 2048], F32, name="o_group", align_bytes=64)
+                    for r in range(GROUP):
+                        st["o", n + r] = (o_group, r * 2048)
             o_sb, base = st["o", n]
             dst = o_sb[:, base + k * 512 : base + (k + 1) * 512]
             if on_scalar:
@@ -279,10 +339,14 @@ def tile_qwen3_5attention_pb_t_kernel(tc, hidden_states, Wq_gate, attn, Wo, out)
                 in_=wo_grp[:, mh * 2048 : (mh + 1) * 2048],
             )
 
+        def warm_up(count):
+            for r in range(count):
+                dummy = ob_pool.tile([P, 512], F32, name="ob")
+                nc.tensor.matmul(out=dummy[:], lhsT=zeros[:, 0:P], rhs=zeros[:], start=True, stop=True)
+
+        warm_up(5)
         transpose_x(0)
-        for r in range(4):
-            dummy = ob_pool.tile([P, 512], F32, name="ob")
-            nc.tensor.matmul(out=dummy[:], lhsT=wq_raw[:, 0:P], rhs=wq_raw[:, 0:512], start=True, stop=True)
+        warm_up(4)
         copy_xt(0, 0, True)
         copy_xt(0, 1, False)
         regroup_wq(0, 0, False)
@@ -338,12 +402,8 @@ def tile_qwen3_5attention_pb_t_kernel(tc, hidden_states, Wq_gate, attn, Wo, out)
             sigmoid(i, 1)
             out_mm(a, 3)
             copy_out(a, 3, False)
-            if a == FIRST - 1:
-                store(a, FIRST)
-            elif FIRST < a < PAIRS and a % 2 == 1:
-                store(a, 2)
-            elif a >= PAIRS:
-                store(a)
+            if a in STORES:
+                store(a, STORES[a])
             transpose_x(d)
             transpose_a(i)
             copy_xt(d, 0, True)
@@ -354,54 +414,56 @@ def tile_qwen3_5attention_pb_t_kernel(tc, hidden_states, Wq_gate, attn, Wo, out)
             quant_x(d)
             quant_g(i)
 
-        u = UNITS - 4
-        copy_out(u, 0, True)
-        copy_out(u, 1, True)
-        store_half(u, 0)
-        copy_out(u, 2, True)
-        gate_mm(u + 2, 0)
-        gate_mm(u + 2, 1)
-        sigmoid(u + 2, 0)
-        sigmoid(u + 2, 1)
-        out_mm(u, 3)
-        copy_out(u, 3, False)
-        store_half(u, 1)
-        transpose_a(u + 2)
-        transpose_a(u + 3)
-        for k in range(3):
-            out_mm(u + 1, k)
-        multiply(u + 2)
-        quant_g(u + 2)
-
-        gate_mm(u + 3, 0)
-        gate_mm(u + 3, 1)
-        copy_out(u + 1, 0, True)
-        copy_out(u + 1, 1, True)
-        store_half(u + 1, 0)
-        copy_out(u + 1, 2, False)
-        sigmoid(u + 3, 0)
-        sigmoid(u + 3, 1)
-        out_mm(u + 1, 3)
-        copy_out(u + 1, 3, False)
-        store_half(u + 1, 1)
-        for k in range(3):
-            out_mm(u + 2, k)
-        multiply(u + 3)
-        quant_g(u + 3)
-
-        copy_out(u + 2, 0, True)
-        copy_out(u + 2, 1, True)
-        store_half(u + 2, 0)
-        out_mm(u + 2, 3, "gt")
-        copy_out(u + 2, 2, True)
-        copy_out(u + 2, 3, False)
-        store_half(u + 2, 1)
-        for k in range(3):
-            out_mm(u + 3, k)
-        out_mm(u + 3, 3, "gt")
-        copy_out(u + 3, 0, True)
-        copy_out(u + 3, 1, False)
-        store_half(u + 3, 0)
-        copy_out(u + 3, 2, True)
-        copy_out(u + 3, 3, False)
-        store_half(u + 3, 1)
+        copy_out(12, 0, True)
+        copy_out(12, 1, True)
+        store_half(12, 0)
+        copy_out(12, 2, True)
+        gate_mm(14, 0)
+        gate_mm(14, 1)
+        sigmoid(14, 0)
+        sigmoid(14, 1)
+        out_mm(12, 3)
+        copy_out(12, 3, False)
+        store_half(12, 1)
+        transpose_a(14)
+        transpose_a(15)
+        out_mm(13, 0)
+        out_mm(13, 1)
+        out_mm(13, 2)
+        out_mm(13, 3, "xt")
+        copy_out(13, 0, True)
+        copy_out(13, 1, True)
+        store_half(13, 0)
+        multiply(14)
+        copy_out(13, 2, True)
+        copy_out(13, 3, False)
+        store_half(13, 1)
+        quant_g(14)
+        gate_mm_half(15, 0)
+        gate_mm_half(15, 1)
+        sigmoid_half(15, 0)
+        sigmoid_half(15, 1)
+        out_mm(14, 0)
+        out_mm(14, 1)
+        out_mm(14, 2)
+        out_mm(14, 3, "at")
+        multiply_half(15, 0)
+        copy_out(14, 0, False)
+        copy_out(14, 1, True)
+        store_half(14, 0)
+        quant_g_half(15, 0)
+        multiply_half(15, 1)
+        copy_out(14, 2, True)
+        copy_out(14, 3, True)
+        store_half(14, 1)
+        quant_g_half(15, 1)
+        out_mm(15, 0)
+        out_mm(15, 1)
+        out_mm(15, 2, "gt")
+        out_mm(15, 3, "gt")
+        copy_out(15, 0, True)
+        copy_out(15, 1, False)
+        store_half(15, 0)
+        copy_out(15, 2, False)
+        copy_out(15, 3, True)
+        store_half(15, 1)

@@ -47,17 +47,17 @@ def tile_qwen3_5attention_pb_t_kernel(tc, hidden_states, Wq_gate, attn, Wo, out)
         warm_out = const.tile([P, 1], F32, name="warm_out")
         nc.vector.memset(warm[:], 0.0)
         nc.scalar.activation(out=warm_out[:], in_=warm[:], func=SIGMOID)
-        ident = const.tile([P, P], F32, name="ident")
+        ident = const.tile([P, P], F32, name="ident", align_bytes=256)
         make_identity(nc, ident[:])
-        zeros = const.tile([P, 512], BF16, name="zeros")
+        zeros = const.tile([P, 512], BF16, name="zeros", align_bytes=256)
         nc.vector.memset(zeros[:], 0.0)
 
-        wqc = const.tile([P, 1024], U32, name="wqc", align_bytes=64)
-        wqs = const.tile([P, 1024], U8, name="wqs", align_bytes=64)
-        woc = const.tile([P, 1024], U32, name="woc", align_bytes=64)
-        wos = const.tile([P, 1024], U8, name="wos", align_bytes=64)
+        wqc = const.tile([P, 1024], U32, name="wqc", align_bytes=256)
+        wqs = const.tile([P, 1024], U8, name="wqs", align_bytes=256)
+        woc = const.tile([P, 1024], U32, name="woc", align_bytes=256)
+        wos = const.tile([P, 1024], U8, name="wos", align_bytes=256)
 
-        staging = first_pool.tile([P, FIRST * 4096], BF16, name="staging", tag="first", align_bytes=64)
+        staging = first_pool.tile([P, FIRST * 4096], BF16, name="staging", tag="first", align_bytes=256)
         wq_raw = staging[:, 0:4096]
         wq_grp = staging[:, 4096:8192]
         wo_raw = staging[:, 8192:12288]
@@ -67,7 +67,7 @@ def tile_qwen3_5attention_pb_t_kernel(tc, hidden_states, Wq_gate, attn, Wo, out)
         x_tiles = []
         first = 0
         for ci, units in enumerate(X_CHUNKS):
-            x_sb = resident.tile([P, units * 2048], BF16, name="x%d" % ci)
+            x_sb = resident.tile([P, units * 2048], BF16, name="x%d" % ci, align_bytes=256)
             x_tiles.append((x_sb, first, units))
             for k in range(units):
                 x_words[first + k] = (x_sb, k * 1024)
@@ -75,7 +75,7 @@ def tile_qwen3_5attention_pb_t_kernel(tc, hidden_states, Wq_gate, attn, Wo, out)
         a_tiles = []
         first = 0
         for ci, units in enumerate(A_CHUNKS):
-            a_sb = resident.tile([P, units * 1024], BF16, name="a%d" % ci)
+            a_sb = resident.tile([P, units * 1024], BF16, name="a%d" % ci, align_bytes=256)
             a_tiles.append((a_sb, first, units))
             for k in range(units):
                 a_words[first + k] = (a_sb, k * 512)
@@ -142,7 +142,7 @@ def tile_qwen3_5attention_pb_t_kernel(tc, hidden_states, Wq_gate, attn, Wo, out)
 
         def copy_xt(n, g, on_scalar):
             if g == 0:
-                xg_new = work.tile([P, 2048], BF16, name="xg", align_bytes=64)
+                xg_new = work.tile([P, 2048], BF16, name="xg", align_bytes=256)
                 st["xg", n] = xg_new
             xg = st["xg", n]
             src = st["xt", n, g][:].rearrange("p (u t) -> p t u", u=2)
@@ -153,8 +153,8 @@ def tile_qwen3_5attention_pb_t_kernel(tc, hidden_states, Wq_gate, attn, Wo, out)
                 nc.vector.tensor_copy(out=dst, in_=src)
 
         def quant_x(n):
-            xc = work.tile([P, 512], U32, name="xc", align_bytes=64)
-            xs = work.tile([P, 512], U8, name="xs", align_bytes=64)
+            xc = work.tile([P, 512], U32, name="xc", align_bytes=256)
+            xs = work.tile([P, 512], U8, name="xs", align_bytes=256)
             nc.vector.quantize_mx(out=xc[:].bitcast(FP8X4), scales=xs[:], in_=st["xg", n][:])
             st["xc", n] = (xc, xs)
 
@@ -196,7 +196,7 @@ def tile_qwen3_5attention_pb_t_kernel(tc, hidden_states, Wq_gate, attn, Wo, out)
 
         def sigmoid_half(n, tt):
             if tt == 0:
-                sig_new = work.tile([P, 1024], F32, name="sig")
+                sig_new = work.tile([P, 1024], F32, name="sig", align_bytes=256)
                 st["sig", n] = sig_new
             nc.scalar.activation(
                 out=st["sig", n][:, tt * 512 : (tt + 1) * 512].rearrange("p (t c e) -> p t c e", c=2, e=2),
@@ -206,7 +206,7 @@ def tile_qwen3_5attention_pb_t_kernel(tc, hidden_states, Wq_gate, attn, Wo, out)
 
         def multiply_half(n, tt):
             if tt == 0:
-                gg_new = work.tile([P, 1024], BF16, name="gg", align_bytes=64)
+                gg_new = work.tile([P, 1024], BF16, name="gg", align_bytes=256)
                 st["gg", n] = gg_new
             at = st["at", n][:].bitcast(BF16).rearrange("p (c t e) -> p t c e", c=2, e=2)
             nc.vector.tensor_tensor(
@@ -218,8 +218,8 @@ def tile_qwen3_5attention_pb_t_kernel(tc, hidden_states, Wq_gate, attn, Wo, out)
 
         def quant_g_half(n, tt):
             if tt == 0:
-                gc_new = work.tile([P, 256], U32, name="gc", align_bytes=64)
-                gs_new = work.tile([P, 256], U8, name="gs", align_bytes=64)
+                gc_new = work.tile([P, 256], U32, name="gc", align_bytes=256)
+                gs_new = work.tile([P, 256], U8, name="gs", align_bytes=256)
                 st["gc", n] = (gc_new, gs_new)
             gc, gs = st["gc", n]
             nc.vector.quantize_mx(
@@ -230,7 +230,7 @@ def tile_qwen3_5attention_pb_t_kernel(tc, hidden_states, Wq_gate, attn, Wo, out)
 
         def sigmoid(n, c):
             if c == 0:
-                sig_new = work.tile([P, 1024], F32, name="sig")
+                sig_new = work.tile([P, 1024], F32, name="sig", align_bytes=256)
                 st["sig", n] = sig_new
             sig = st["sig", n]
             nc.scalar.activation(
@@ -240,7 +240,7 @@ def tile_qwen3_5attention_pb_t_kernel(tc, hidden_states, Wq_gate, attn, Wo, out)
             )
 
         def multiply(n):
-            gg = work.tile([P, 1024], BF16, name="gg", align_bytes=64)
+            gg = work.tile([P, 1024], BF16, name="gg", align_bytes=256)
             nc.vector.tensor_tensor(
                 out=gg[:].rearrange("p (t c e) -> p t c e", c=2, e=2),
                 in0=st["sig", n][:].rearrange("p (c t e) -> p t c e", c=2, e=2),
@@ -250,8 +250,8 @@ def tile_qwen3_5attention_pb_t_kernel(tc, hidden_states, Wq_gate, attn, Wo, out)
             st["gg", n] = gg
 
         def quant_g(n):
-            gc = work.tile([P, 256], U32, name="gc", align_bytes=64)
-            gs = work.tile([P, 256], U8, name="gs", align_bytes=64)
+            gc = work.tile([P, 256], U32, name="gc", align_bytes=256)
+            gs = work.tile([P, 256], U8, name="gs", align_bytes=256)
             nc.vector.quantize_mx(out=gc[:].bitcast(FP8X4), scales=gs[:], in_=st["gg", n][:])
             st["gc", n] = (gc, gs)
 
@@ -280,11 +280,11 @@ def tile_qwen3_5attention_pb_t_kernel(tc, hidden_states, Wq_gate, attn, Wo, out)
         def copy_out(n, k, on_scalar):
             if k == 0:
                 if n == 0:
-                    o_first = first_pool.tile([P, FIRST * 2048], F32, name="o_first", tag="first", align_bytes=64)
+                    o_first = first_pool.tile([P, FIRST * 2048], F32, name="o_first", tag="first", align_bytes=256)
                     for r in range(FIRST):
                         st["o", r] = (o_first, r * 2048)
                 elif n >= FIRST and (n - FIRST) % GROUP == 0:
-                    o_group = group_pool.tile([P, GROUP * 2048], F32, name="o_group", align_bytes=64)
+                    o_group = group_pool.tile([P, GROUP * 2048], F32, name="o_group", align_bytes=256)
                     for r in range(GROUP):
                         st["o", n + r] = (o_group, r * 2048)
             o_sb, base = st["o", n]

@@ -14,20 +14,27 @@ SIGMOID = mybir.ActivationFunctionType.Sigmoid
 MULT = mybir.AluOpType.mult
 
 P = 128
-TILES = 32
+BLOCK = 8
 UNITS = 16
-X_CHUNKS = (1, 1, 1, 1, 2, 4, 6)
+X_CHUNKS = (1, 1, 1, 1, 2, 2, 8)
 A_CHUNKS = (1, 3, 4, 8)
-FIRST = 5
-GROUP = 3
-STORES = {4: 5, 7: 3, 9: 2, 10: 1, 11: 1}
+FIRST = 4
+GROUP = 4
+STORES = {3: 4, 6: 3, 7: 1, 9: 2, 10: 1, 11: 1}
 
 
 def tile_qwen3_5attention_pb_t_kernel(tc, hidden_states, Wq_gate, attn, Wo, out):
     nc = tc.nc
-    x_v = hidden_states.flatten_outer_dims().rearrange("(p j) m -> p j m", j=TILES)
-    a_v = attn.rearrange("b s u h -> (b s) (u h)").rearrange("(p j) e -> p j e", j=TILES)
-    o_v = out.flatten_outer_dims().rearrange("(p j) m -> p j m", j=TILES)
+    x_v = hidden_states.flatten_outer_dims().rearrange("(b p j) m -> b p j m", p=P, j=BLOCK)
+    a_v = attn.rearrange("b s u h -> (b s) (u h)").rearrange("(b p j) e -> b p j e", p=P, j=BLOCK)
+    o_v = out.flatten_outer_dims().rearrange("(b p j) m -> b p j m", p=P, j=BLOCK)
+
+    def tiles_of(view, first, count):
+        b, j = divmod(first, BLOCK)
+        if count <= BLOCK - j:
+            return view[b, :, j : j + count, :]
+        return view[b : b + count // BLOCK, :, :, :].rearrange("b p j m -> p b (j m)")
+
     wq_v = Wq_gate.rearrange("(a q e) u h -> q a (e u h)", a=4, q=P, e=2)
     wo_v = Wo.rearrange("u h m -> (u h) m").rearrange("(c q e) m -> q c (e m)", c=2, q=P, e=2)
 
@@ -83,17 +90,19 @@ def tile_qwen3_5attention_pb_t_kernel(tc, hidden_states, Wq_gate, attn, Wo, out)
 
         def load_x(ci):
             x_sb, u0, units = x_tiles[ci]
-            nc.sync.dma_start(
-                out=x_sb[:].rearrange("p (j m) -> p j m", j=2 * units),
-                in_=x_v[:, 2 * u0 : 2 * (u0 + units), :],
-            )
+            if units <= BLOCK // 2:
+                dst = x_sb[:].rearrange("p (j m) -> p j m", j=2 * units)
+            else:
+                dst = x_sb[:].rearrange("p (b n) -> p b n", b=2 * units // BLOCK)
+            nc.sync.dma_start(out=dst, in_=tiles_of(x_v, 2 * u0, 2 * units))
 
         def load_a(ci):
             a_sb, u0, units = a_tiles[ci]
-            nc.sync.dma_start(
-                out=a_sb[:].rearrange("p (j e) -> p j e", j=2 * units),
-                in_=a_v[:, 2 * u0 : 2 * (u0 + units), :],
-            )
+            if units <= BLOCK // 2:
+                dst = a_sb[:].rearrange("p (j m) -> p j m", j=2 * units)
+            else:
+                dst = a_sb[:].rearrange("p (b n) -> p b n", b=2 * units // BLOCK)
+            nc.sync.dma_start(out=dst, in_=tiles_of(a_v, 2 * u0, 2 * units))
 
         load_x(0)
         for g in range(2):
@@ -107,10 +116,11 @@ def tile_qwen3_5attention_pb_t_kernel(tc, hidden_states, Wq_gate, attn, Wo, out)
         load_x(2)
         load_x(3)
         load_a(1)
-        for ci in range(4, len(X_CHUNKS)):
-            load_x(ci)
-            if ci < len(X_CHUNKS) - 1:
-                load_a(ci - 2)
+        load_x(4)
+        load_a(2)
+        load_x(5)
+        load_x(6)
+        load_a(3)
 
         st = {}
 
@@ -297,15 +307,15 @@ def tile_qwen3_5attention_pb_t_kernel(tc, hidden_states, Wq_gate, attn, Wo, out)
         def store(n, units=1):
             o_sb, base = st["o", n - units + 1]
             nc.sync.dma_start(
-                out=o_v[:, 2 * (n - units + 1) : 2 * n + 2, :],
+                out=tiles_of(o_v, 2 * (n - units + 1), 2 * units),
                 in_=o_sb[:, base : base + units * 2048].rearrange("p (j m) -> p j m", j=2 * units),
             )
 
         def store_half(n, tt):
             o_sb, base = st["o", n]
             nc.sync.dma_start(
-                out=o_v[:, 2 * n + tt, :],
-                in_=o_sb[:, base + tt * 1024 : base + (tt + 1) * 1024],
+                out=tiles_of(o_v, 2 * n + tt, 1),
+                in_=o_sb[:, base + tt * 1024 : base + (tt + 1) * 1024].rearrange("p (j m) -> p j m", j=1),
             )
 
         def regroup_wq(g, e, on_scalar):

@@ -318,6 +318,13 @@ def tile_qwen3_5attention_pb_t_kernel(tc, hidden_states, Wq_gate, attn, Wo, out)
                 in_=o_sb[:, base + tt * 1024 : base + (tt + 1) * 1024].rearrange("p (j m) -> p j m", j=1),
             )
 
+        def store_quarter(n, k):
+            o_sb, base = st["o", n]
+            nc.sync.dma_start(
+                out=tiles_of(o_v, 2 * n + k // 2, 1)[:, :, (k % 2) * 512 : (k % 2 + 1) * 512],
+                in_=o_sb[:, base + k * 512 : base + (k + 1) * 512].rearrange("p (j m) -> p j m", j=1),
+            )
+
         def regroup_wq(g, e, on_scalar):
             src = wq_raw[:, g * 2048 : (g + 1) * 2048].rearrange("p (j n e) -> p e n j", j=4, e=2)[:, e, :, :]
             dst = wq_grp[:, g * 2048 + e * 1024 : g * 2048 + (e + 1) * 1024].rearrange("p (n j) -> p n j", j=4)
@@ -475,5 +482,6 @@ def tile_qwen3_5attention_pb_t_kernel(tc, hidden_states, Wq_gate, attn, Wo, out)
         copy_out(15, 1, False)
         store_half(15, 0)
         copy_out(15, 2, False)
+        store_quarter(15, 2)
         copy_out(15, 3, True)
-        store_half(15, 1)
+        store_quarter(15, 3)

from contextlib import ExitStack

import concourse.mybir as mybir
from concourse.masks import make_identity

FLOPS = 2 * 4096 * 1024 * 512 * 2

BF16 = mybir.dt.bfloat16
F32 = mybir.dt.float32
U32 = mybir.dt.uint32
U8 = mybir.dt.uint8
FP8X4 = mybir.dt.float8_e4m3fn_x4
SIGMOID = mybir.ActivationFunctionType.Sigmoid
MULT = mybir.AluOpType.mult

P = 128
BLOCK = 8
UNITS = 16
X_CHUNKS = (1, 1, 1, 1, 2, 2, 8)
A_CHUNKS = (1, 3, 4, 8)
FIRST = 4
GROUP = 4
STORES = {3: 4, 6: 3, 7: 1, 9: 2, 10: 1, 11: 1}


def tile_qwen3_5attention_pb_t_kernel(tc, hidden_states, Wq_gate, attn, Wo, out):
    nc = tc.nc
    x_v = hidden_states.flatten_outer_dims().rearrange("(b p j) m -> b p j m", p=P, j=BLOCK)
    a_v = attn.rearrange("b s u h -> (b s) (u h)").rearrange("(b p j) e -> b p j e", p=P, j=BLOCK)
    o_v = out.flatten_outer_dims().rearrange("(b p j) m -> b p j m", p=P, j=BLOCK)

    def tiles_of(view, first, count):
        b, j = divmod(first, BLOCK)
        if count <= BLOCK - j:
            return view[b, :, j : j + count, :]
        return view[b : b + count // BLOCK, :, :, :].rearrange("b p j m -> p b (j m)")

    wq_v = Wq_gate.rearrange("(a q e) u h -> q a (e u h)", a=4, q=P, e=2)
    wo_v = Wo.rearrange("u h m -> (u h) m").rearrange("(c q e) m -> q c (e m)", c=2, q=P, e=2)

    with ExitStack() as ctx:
        const = ctx.enter_context(tc.tile_pool(name="const", bufs=1))
        resident = ctx.enter_context(tc.tile_pool(name="resident", bufs=1))
        first_pool = ctx.enter_context(tc.tile_pool(name="first", bufs=1))
        group_pool = ctx.enter_context(tc.tile_pool(name="group", bufs=2))
        work = ctx.enter_context(tc.tile_pool(name="work", bufs=2))
        xt_pool = ctx.enter_context(tc.psum_pool(name="xt", bufs=2))
        at_pool = ctx.enter_context(tc.psum_pool(name="at", bufs=1))
        gate_pool = ctx.enter_context(tc.psum_pool(name="gate", bufs=2))
        ob_pool = ctx.enter_context(tc.psum_pool(name="ob", bufs=3))
        ctx.enter_context(tc.manual_schedule())

        warm = const.tile([P, 1], F32, name="warm")
        warm_out = const.tile([P, 1], F32, name="warm_out")
        nc.vector.memset(warm[:], 0.0)
        nc.scalar.activation(out=warm_out[:], in_=warm[:], func=SIGMOID)
        ident = const.tile([P, P], F32, name="ident", align_bytes=256)
        make_identity(nc, ident[:])
        zeros = const.tile([P, 512], BF16, name="zeros", align_bytes=256)
        nc.vector.memset(zeros[:], 0.0)

        wqc = const.tile([P, 1024], U32, name="wqc", align_bytes=256)
        wqs = const.tile([P, 1024], U8, name="wqs", align_bytes=256)
        woc = const.tile([P, 1024], U32, name="woc", align_bytes=256)
        wos = const.tile([P, 1024], U8, name="wos", align_bytes=256)

        staging = first_pool.tile([P, FIRST * 4096], BF16, name="staging", tag="first", align_bytes=256)
        wq_raw = staging[:, 0:4096]
        wq_grp = staging[:, 4096:8192]
        wo_raw = staging[:, 8192:12288]
        wo_grp = staging[:, 12288:16384]
        x_words = {}
        a_words = {}
        x_tiles = []
        first = 0
        for ci, units in enumerate(X_CHUNKS):
            x_sb = resident.tile([P, units * 2048], BF16, name="x%d" % ci, align_bytes=256)
            x_tiles.append((x_sb, first, units))
            for k in range(units):
                x_words[first + k] = (x_sb, k * 1024)
            first += units
        a_tiles = []
        first = 0
        for ci, units in enumerate(A_CHUNKS):
            a_sb = resident.tile([P, units * 1024], BF16, name="a%d" % ci, align_bytes=256)
            a_tiles.append((a_sb, first, units))
            for k in range(units):
                a_words[first + k] = (a_sb, k * 512)
            first += units

        def load_x(ci):
            x_sb, u0, units = x_tiles[ci]
            if units <= BLOCK // 2:
                dst = x_sb[:].rearrange("p (j m) -> p j m", j=2 * units)
            else:
                dst = x_sb[:].rearrange("p (b n) -> p b n", b=2 * units // BLOCK)
            nc.sync.dma_start(out=dst, in_=tiles_of(x_v, 2 * u0, 2 * units))

        def load_a(ci):
            a_sb, u0, units = a_tiles[ci]
            if units <= BLOCK // 2:
                dst = a_sb[:].rearrange("p (j m) -> p j m", j=2 * units)
            else:
                dst = a_sb[:].rearrange("p (b n) -> p b n", b=2 * units // BLOCK)
            nc.sync.dma_start(out=dst, in_=tiles_of(a_v, 2 * u0, 2 * units))

        load_x(0)
        for g in range(2):
            nc.sync.dma_start(
                out=wq_raw[:, g * 2048 : (g + 1) * 2048].rearrange("p (a n) -> p a n", a=2),
                in_=wq_v[:, 2 * g : 2 * g + 2, :],
            )
        load_x(1)
        nc.sync.dma_start(out=wo_raw.rearrange("p (c n) -> p c n", c=2), in_=wo_v)
        load_a(0)
        load_x(2)
        load_x(3)
        load_a(1)
        load_x(4)
        load_a(2)
        load_x(5)
        load_x(6)
        load_a(3)

        st = {}

        def transpose_x(n):
            x_sb, base = x_words[n]
            xw = x_sb[:].bitcast(F32)
            for g in range(2):
                xt = xt_pool.tile([P, 512], F32, name="xt")
                for u in range(2):
                    for tt in range(2):
                        col = base + tt * 512 + (2 * g + u) * P
                        dst = u * 256 + tt * P
                        nc.tensor.transpose(xt[:, dst : dst + P], xw[:, col : col + P], ident[:])
                st["xt", n, g] = xt

        def transpose_a(n):
            a_sb, base = a_words[n]
            aw = a_sb[:].bitcast(F32)
            if n == UNITS - 1:
                at = xt_pool.tile([P, 512], F32, name="xt")
            else:
                at = at_pool.tile([P, 512], F32, name="at")
            for c in range(2):
                for tt in range(2):
                    col = base + tt * 256 + c * P
                    dst = c * 256 + tt * P
                    nc.tensor.transpose(at[:, dst : dst + P], aw[:, col : col + P], ident[:])
            st["at", n] = at

        def copy_xt(n, g, on_scalar):
            if g == 0:
                xg_new = work.tile([P, 2048], BF16, name="xg", align_bytes=256)
                st["xg", n] = xg_new
            xg = st["xg", n]
            src = st["xt", n, g][:].rearrange("p (u t) -> p t u", u=2)
            dst = xg[:].bitcast(F32)[:, g * 512 : (g + 1) * 512].rearrange("p (t u) -> p t u", u=2)
            if on_scalar:
                nc.scalar.copy(out=dst, in_=src)
            else:
                nc.vector.tensor_copy(out=dst, in_=src)

        def quant_x(n):
            xc = work.tile([P, 512], U32, name="xc", align_bytes=256)
            xs = work.tile([P, 512], U8, name="xs", align_bytes=256)
            nc.vector.quantize_mx(out=xc[:].bitcast(FP8X4), scales=xs[:], in_=st["xg", n][:])
            st["xc", n] = (xc, xs)

        def gate_mm(n, c):
            xc, xs = st["xc", n]
            gt = gate_pool.tile([P, 512], F32, name="gt")
            for e in range(2):
                for g in range(2):
                    w0 = g * 512 + (e * 2 + c) * P
                    nc.tensor.matmul_mx(
                        out=gt[:, e * 256 : (e + 1) * 256],
                        lhsT=wqc[:, w0 : w0 + P].bitcast(FP8X4),
                        lhsT_scale=wqs[:, w0 : w0 + P],
                        rhs=xc[:, g * 256 : (g + 1) * 256].bitcast(FP8X4),
                        rhs_scale=xs[:, g * 256 : (g + 1) * 256],
                        start=(g == 0),
                        stop=(g == 1),
                    )
            st["gt", n, c] = gt

        def gate_mm_half(n, tt):
            xc, xs = st["xc", n]
            gt = gate_pool.tile([P, 512], F32, name="gt")
            for c in range(2):
                for e in range(2):
                    for g in range(2):
                        w0 = g * 512 + (e * 2 + c) * P
                        t0 = g * 256 + tt * P
                        nc.tensor.matmul_mx(
                            out=gt[:, (2 * c + e) * P : (2 * c + e + 1) * P],
                            lhsT=wqc[:, w0 : w0 + P].bitcast(FP8X4),
                            lhsT_scale=wqs[:, w0 : w0 + P],
                            rhs=xc[:, t0 : t0 + P].bitcast(FP8X4),
                            rhs_scale=xs[:, t0 : t0 + P],
                            start=(g == 0),
                            stop=(g == 1),
                        )
            st["gt", n, tt] = gt

        def sigmoid_half(n, tt):
            if tt == 0:
                sig_new = work.tile([P, 1024], F32, name="sig", align_bytes=256)
                st["sig", n] = sig_new
            nc.scalar.activation(
                out=st["sig", n][:, tt * 512 : (tt + 1) * 512].rearrange("p (t c e) -> p t c e", c=2, e=2),
                in_=st["gt", n, tt][:].rearrange("p (c e t) -> p t c e", c=2, e=2),
                func=SIGMOID,
            )

        def multiply_half(n, tt):
            if tt == 0:
                gg_new = work.tile([P, 1024], BF16, name="gg", align_bytes=256)
                st["gg", n] = gg_new
            at = st["at", n][:].bitcast(BF16).rearrange("p (c t e) -> p t c e", c=2, e=2)
            nc.vector.tensor_tensor(
                out=st["gg", n][:, tt * 512 : (tt + 1) * 512].rearrange("p (t c e) -> p t c e", c=2, e=2),
                in0=st["sig", n][:, tt * 512 : (tt + 1) * 512].rearrange("p (t c e) -> p t c e", c=2, e=2),
                in1=at[:, tt * P : (tt + 1) * P, :, :],
                op=MULT,
            )

        def quant_g_half(n, tt):
            if tt == 0:
                gc_new = work.tile([P, 256], U32, name="gc", align_bytes=256)
                gs_new = work.tile([P, 256], U8, name="gs", align_bytes=256)
                st["gc", n] = (gc_new, gs_new)
            gc, gs = st["gc", n]
            nc.vector.quantize_mx(
                out=gc[:, tt * P : (tt + 1) * P].bitcast(FP8X4),
                scales=gs[:, tt * P : (tt + 1) * P],
                in_=st["gg", n][:, tt * 512 : (tt + 1) * 512],
            )

        def sigmoid(n, c):
            if c == 0:
                sig_new = work.tile([P, 1024], F32, name="sig", align_bytes=256)
                st["sig", n] = sig_new
            sig = st["sig", n]
            nc.scalar.activation(
                out=sig[:, c * 512 : (c + 1) * 512].rearrange("p (t e) -> p t e", e=2),
                in_=st["gt", n, c][:].rearrange("p (e t) -> p t e", e=2),
                func=SIGMOID,
            )

        def multiply(n):
            gg = work.tile([P, 1024], BF16, name="gg", align_bytes=256)
            nc.vector.tensor_tensor(
                out=gg[:].rearrange("p (t c e) -> p t c e", c=2, e=2),
                in0=st["sig", n][:].rearrange("p (c t e) -> p t c e", c=2, e=2),
                in1=st["at", n][:].bitcast(BF16).rearrange("p (c t e) -> p t c e", c=2, e=2),
                op=MULT,
            )
            st["gg", n] = gg

        def quant_g(n):
            gc = work.tile([P, 256], U32, name="gc", align_bytes=256)
            gs = work.tile([P, 256], U8, name="gs", align_bytes=256)
            nc.vector.quantize_mx(out=gc[:].bitcast(FP8X4), scales=gs[:], in_=st["gg", n][:])
            st["gc", n] = (gc, gs)

        def out_mm(n, k, bank="ob"):
            gc, gs = st["gc", n]
            tt, mh = divmod(k, 2)
            if bank == "gt":
                ob = gate_pool.tile([P, 512], F32, name="gt")
            elif bank == "xt":
                ob = xt_pool.tile([P, 512], F32, name="xt")
            elif bank == "at":
                ob = at_pool.tile([P, 512], F32, name="at")
            else:
                ob = ob_pool.tile([P, 512], F32, name="ob")
            nc.tensor.matmul_mx(
                out=ob[:],
                lhsT=gc[:, tt * P : (tt + 1) * P].bitcast(FP8X4),
                lhsT_scale=gs[:, tt * P : (tt + 1) * P],
                rhs=woc[:, mh * 512 : (mh + 1) * 512].bitcast(FP8X4),
                rhs_scale=wos[:, mh * 512 : (mh + 1) * 512],
                start=True,
                stop=True,
            )
            st["ob", n, k] = ob

        def copy_out(n, k, on_scalar):
            if k == 0:
                if n == 0:
                    o_first = first_pool.tile([P, FIRST * 2048], F32, name="o_first", tag="first", align_bytes=256)
                    for r in range(FIRST):
                        st["o", r] = (o_first, r * 2048)
                elif n >= FIRST and (n - FIRST) % GROUP == 0:
                    o_group = group_pool.tile([P, GROUP * 2048], F32, name="o_group", align_bytes=256)
                    for r in range(GROUP):
                        st["o", n + r] = (o_group, r * 2048)
            o_sb, base = st["o", n]
            dst = o_sb[:, base + k * 512 : base + (k + 1) * 512]
            if on_scalar:
                nc.scalar.copy(out=dst, in_=st["ob", n, k][:])
            else:
                nc.vector.tensor_copy(out=dst, in_=st["ob", n, k][:])

        def store(n, units=1):
            o_sb, base = st["o", n - units + 1]
            nc.sync.dma_start(
                out=tiles_of(o_v, 2 * (n - units + 1), 2 * units),
                in_=o_sb[:, base : base + units * 2048].rearrange("p (j m) -> p j m", j=2 * units),
            )

        def store_half(n, tt):
            o_sb, base = st["o", n]
            nc.sync.dma_start(
                out=tiles_of(o_v, 2 * n + tt, 1),
                in_=o_sb[:, base + tt * 1024 : base + (tt + 1) * 1024].rearrange("p (j m) -> p j m", j=1),
            )

        def store_quarter(n, k):
            o_sb, base = st["o", n]
            nc.sync.dma_start(
                out=tiles_of(o_v, 2 * n + k // 2, 1)[:, :, (k % 2) * 512 : (k % 2 + 1) * 512],
                in_=o_sb[:, base + k * 512 : base + (k + 1) * 512].rearrange("p (j m) -> p j m", j=1),
            )

        def regroup_wq(g, e, on_scalar):
            src = wq_raw[:, g * 2048 : (g + 1) * 2048].rearrange("p (j n e) -> p e n j", j=4, e=2)[:, e, :, :]
            dst = wq_grp[:, g * 2048 + e * 1024 : g * 2048 + (e + 1) * 1024].rearrange("p (n j) -> p n j", j=4)
            if on_scalar:
                nc.scalar.copy(out=dst, in_=src)
            else:
                nc.vector.tensor_copy(out=dst, in_=src)

        def quant_wq(g):
            nc.vector.quantize_mx(
                out=wqc[:, g * 512 : (g + 1) * 512].bitcast(FP8X4),
                scales=wqs[:, g * 512 : (g + 1) * 512],
                in_=wq_grp[:, g * 2048 : (g + 1) * 2048],
            )

        def regroup_wo(mh, on_scalar):
            rows = wo_raw.rearrange("p (j m) -> p j m", j=4)[:, :, mh * 512 : (mh + 1) * 512]
            src = rows.rearrange("p j (c i) -> p c j i", i=4)
            dst = wo_grp[:, mh * 2048 : (mh + 1) * 2048].rearrange("p (c i j) -> p c j i", i=4, j=4)
            if on_scalar:
                nc.scalar.copy(out=dst, in_=src)
            else:
                nc.vector.tensor_copy(out=dst, in_=src)

        def quant_wo(mh):
            nc.vector.quantize_mx(
                out=woc[:, mh * 512 : (mh + 1) * 512].bitcast(FP8X4),
                scales=wos[:, mh * 512 : (mh + 1) * 512],
                in_=wo_grp[:, mh * 2048 : (mh + 1) * 2048],
            )

        def warm_up(count):
            for r in range(count):
                dummy = ob_pool.tile([P, 512], F32, name="ob")
                nc.tensor.matmul(out=dummy[:], lhsT=zeros[:, 0:P], rhs=zeros[:], start=True, stop=True)

        warm_up(5)
        transpose_x(0)
        warm_up(4)
        copy_xt(0, 0, True)
        copy_xt(0, 1, False)
        regroup_wq(0, 0, False)
        regroup_wq(0, 1, True)
        quant_x(0)
        regroup_wq(1, 0, False)
        regroup_wq(1, 1, True)
        quant_wq(0)
        transpose_x(1)
        copy_xt(1, 0, True)
        copy_xt(1, 1, True)
        quant_wq(1)
        quant_x(1)
        gate_mm(0, 0)
        gate_mm(0, 1)
        sigmoid(0, 0)
        sigmoid(0, 1)
        transpose_a(0)
        regroup_wo(0, False)
        regroup_wo(1, True)
        gate_mm(1, 0)
        gate_mm(1, 1)
        multiply(0)
        quant_wo(0)
        quant_g(0)
        transpose_x(2)
        copy_xt(2, 0, True)
        copy_xt(2, 1, False)
        sigmoid(1, 0)
        sigmoid(1, 1)
        quant_wo(1)
        quant_x(2)
        out_mm(0, 0)
        out_mm(0, 2)
        transpose_x(3)
        transpose_a(1)
        copy_xt(3, 0, True)
        copy_xt(3, 1, False)
        out_mm(0, 1)
        multiply(1)
        quant_x(3)
        quant_g(1)
        for i in range(2, UNITS - 2):
            a = i - 2
            b = i - 1
            d = i + 2
            copy_out(a, 0, True)
            copy_out(a, 1, True)
            copy_out(a, 2, True)
            gate_mm(i, 0)
            gate_mm(i, 1)
            sigmoid(i, 0)
            sigmoid(i, 1)
            out_mm(a, 3)
            copy_out(a, 3, False)
            if a in STORES:
                store(a, STORES[a])
            transpose_x(d)
            transpose_a(i)
            copy_xt(d, 0, True)
            copy_xt(d, 1, False)
            for k in range(3):
                out_mm(b, k)
            multiply(i)
            quant_x(d)
            quant_g(i)

        copy_out(12, 0, True)
        copy_out(12, 1, True)
        store_half(12, 0)
        copy_out(12, 2, True)
        gate_mm(14, 0)
        gate_mm(14, 1)
        sigmoid(14, 0)
        sigmoid(14, 1)
        out_mm(12, 3)
        copy_out(12, 3, False)
        store_half(12, 1)
        transpose_a(14)
        transpose_a(15)
        out_mm(13, 0)
        out_mm(13, 1)
        out_mm(13, 2)
        out_mm(13, 3, "xt")
        copy_out(13, 0, True)
        copy_out(13, 1, True)
        store_half(13, 0)
        multiply(14)
        copy_out(13, 2, True)
        copy_out(13, 3, False)
        store_half(13, 1)
        quant_g(14)
        gate_mm_half(15, 0)
        gate_mm_half(15, 1)
        sigmoid_half(15, 0)
        sigmoid_half(15, 1)
        out_mm(14, 0)
        out_mm(14, 1)
        out_mm(14, 2)
        out_mm(14, 3, "at")
        multiply_half(15, 0)
        copy_out(14, 0, False)
        copy_out(14, 1, True)
        store_half(14, 0)
        quant_g_half(15, 0)
        multiply_half(15, 1)
        copy_out(14, 2, True)
        copy_out(14, 3, True)
        store_half(14, 1)
        quant_g_half(15, 1)
        out_mm(15, 0)
        out_mm(15, 1)
        out_mm(15, 2, "gt")
        out_mm(15, 3, "gt")
        copy_out(15, 0, True)
        copy_out(15, 1, False)
        store_half(15, 0)
        copy_out(15, 2, False)
        store_quarter(15, 2)
        copy_out(15, 3, True)
        store_quarter(15, 3)
